import numpy as np
import ml_dtypes


def mxq(x, axis, fmt="e4m3"):
    dtype, down = {"e4m3": (ml_dtypes.float8_e4m3fn, 7), "e5m2": (ml_dtypes.float8_e5m2, 14)}[fmt]
    v = np.moveaxis(np.asarray(x, np.float32).astype(ml_dtypes.bfloat16).astype(np.float64), axis, -1)
    blocks = v.reshape(v.shape[:-1] + (-1, 32))
    amax = np.abs(blocks).max(-1, keepdims=True)
    byte = np.maximum(np.where(amax > 0, np.frexp(amax)[1] - 1 + 127, 0) - down, 1)
    scale = np.exp2(byte - 127.0)
    codes = (blocks / scale).astype(np.float32).astype(dtype).astype(np.float64)
    return np.moveaxis((codes * scale).reshape(v.shape), -1, axis)


WIDE = False


def mx_kscale(k):
    if not WIDE:
        return np.ones(k)
    levels = np.array([10, -10, 5, -5, 0])
    if k % 512:
        return np.exp2(np.random.permutation(np.resize(levels, k // 32))).repeat(32)
    a = np.empty((k // 512, 16))
    for p in range(k // 512):
        a[p, :8] = np.random.permutation(np.resize(levels, 8))
        for g in range(8):
            far = levels[np.abs(levels - a[p, g]) >= 10]
            a[p, g + 8] = far[np.random.randint(len(far))]
    return np.exp2(a.ravel()).repeat(32)


BF16 = ml_dtypes.bfloat16


def bf(x):
    return np.asarray(x, np.float32).astype(BF16)


def f64(x):
    return np.asarray(x).astype(np.float64)


NB, D, CO, CV, R = 16, 256, 128, 512, 512


def setup_inputs():
    s, t = mx_kscale(CV), mx_kscale(R)
    return {"x1": bf(np.random.standard_normal((NB, D, CO))),
            "A": bf(np.random.standard_normal((D, R)) / np.sqrt(D) * t),
            "t2": bf(np.random.standard_normal((NB, R, CV)) * s),
            "w": bf(np.random.standard_normal((NB, CO, CV)) / np.sqrt(CV) / s),
            "C": bf(np.random.standard_normal((D, R)) / np.sqrt(R) / t)}


def reference(x1, A, t2, w, C):
    t1 = f64(A).T @ f64(x1)
    t3 = mxq(f64(t2), 2, "e4m3") @ mxq(f64(w).transpose(0, 2, 1), 1, "e4m3")
    h = t1 * t3
    return mxq(f64(C), 1, "e4m3") @ mxq(h, 1, "e4m3")

@@ -1,0 +1,213 @@
+from contextlib import ExitStack
+
+import concourse.mybir as mybir
+from concourse.masks import make_identity
+
+NB, D, CO, CV, R = 16, 256, 128, 512, 512
+FLOPS = 2 * NB * CO * (R * D + R * CV + D * R)
+
+F32 = mybir.dt.float32
+BF16 = mybir.dt.bfloat16
+U32 = mybir.dt.uint32
+U8 = mybir.dt.uint8
+FP8X4 = mybir.dt.float8_e4m3fn_x4
+T3_DT = F32
+
+P = 128
+LOOKAHEAD = 2
+
+
+def tile_cptensorproduct_pa_kernel(tc, x1, A, t2, w, C, out):
+    nc = tc.nc
+    with ExitStack() as ctx:
+        keep = ctx.enter_context(tc.tile_pool(name="keep", bufs=1))
+        work = ctx.enter_context(tc.tile_pool(name="work", bufs=3))
+        psum = ctx.enter_context(tc.psum_pool(name="psum", bufs=1))
+        ctx.enter_context(tc.manual_schedule())
+
+        t2_sb = [keep.tile([P, 4 * CV], BF16, name="t2_sb%d" % b, tag="t2_sb%d" % b) for b in range(NB)]
+        w_sb = [keep.tile([P, 2, CV], BF16, name="w_sb%d" % k, tag="w_sb%d" % k) for k in range(NB // 2)]
+        x1_sb = [keep.tile([P, 4, 2 * CO], BF16, name="x1_sb%d" % g, tag="x1_sb%d" % g) for g in range(NB // 4)]
+        a_raw = keep.tile([P, 2 * R], BF16, name="a_raw", tag="a_raw")
+        c_raw = keep.tile([P, 2 * R], BF16, name="c_raw", tag="c_raw")
+
+        def load_w(k):
+            nc.sync.dma_start(out=w_sb[k][:], in_=w[2 * k : 2 * k + 2].rearrange("b c k -> c b k"))
+
+        load_w(0)
+        for b in range(NB):
+            nc.sync.dma_start(out=t2_sb[b][:], in_=t2[b].rearrange("(m t) k -> m (t k)", t=4))
+            if b % 2 == 0 and b // 2 + 1 < NB // 2:
+                load_w(b // 2 + 1)
+            if b == 1:
+                nc.sync.dma_start(out=a_raw[:], in_=A.rearrange("(p e) r -> p (e r)", e=2))
+            if b % 4 == 1:
+                g = b // 4
+                nc.sync.dma_start(
+                    out=x1_sb[g][:], in_=x1[4 * g : 4 * g + 4].rearrange("b (p e) c -> p b (e c)", e=2)
+                )
+            if b == 3:
+                nc.sync.dma_start(out=c_raw[:], in_=C.rearrange("(p e) r -> p (e r)", e=2))
+
+        ident = keep.tile([P, P], F32, name="ident", tag="ident")
+        make_identity(nc, ident[:])
+        a_perm = keep.tile([P, 2, 4, P], BF16, name="a_perm", tag="a_perm")
+        c_grouped = keep.tile([P, 4 * D], BF16, name="c_grouped", tag="c_grouped", align_bytes=64)
+        c_codes = keep.tile([P, D], U32, name="c_codes", tag="c_codes", align_bytes=64)
+        c_scales = keep.tile([P, D], U8, name="c_scales", tag="c_scales", align_bytes=64)
+
+        def half(words, h, grouped):
+            bank = psum.tile([P, 2, 2, P], F32, name="tp", tag="tp", bufs=5)
+            trs = []
+            for s in (0, 1):
+                for u in (0, 1):
+                    lo = 256 * (2 * h + s)
+                    trs.append((bank[:, s, u, :], words[:, lo + u : lo + 256 : 2]))
+            dst = grouped[:].bitcast(F32)[:, 512 * h : 512 * (h + 1)].rearrange("p (s m u) -> p s m u", s=2, u=2)
+            return trs, (dst, bank[:].rearrange("p s u m -> p s m u"))
+
+        def quantize(grouped, codes, scales):
+            nc.vector.quantize_mx(out=codes[:].bitcast(FP8X4), scales=scales[:], in_=grouped[:])
+
+        def weave(mms, trs):
+            for o, i in trs if not mms else []:
+                nc.tensor.transpose(o, i, ident[:])
+            gaps = len(mms) - 1
+            for n, (o, l, r, first, last) in enumerate(mms):
+                nc.tensor.matmul(o, lhsT=l, rhs=r, start=first, stop=last)
+                if n < gaps:
+                    for o2, i2 in trs[len(trs) * n // gaps : len(trs) * (n + 1) // gaps]:
+                        nc.tensor.transpose(o2, i2, ident[:])
+
+        t2_q = {}
+        w_q = {}
+        h_grouped = {}
+        h_q = {}
+        t1_ps = {}
+        t3_sb = {}
+
+        for i in range(-3, NB + 3):
+            j = i + LOOKAHEAD
+            trs = []
+            copies = []
+            quants = []
+            if i % 2 == 1 and (i + 3) // 2 < NB // 2:
+                k = (i + 3) // 2
+                wg = work.tile([P, 4 * 2 * CO], BF16, name="wg", tag="wg", align_bytes=64)
+                wc = work.tile([P, 2 * CO], U32, name="wc", tag="wc", align_bytes=64)
+                ws = work.tile([P, 2 * CO], U8, name="ws", tag="ws", align_bytes=64)
+                t, c = half(w_sb[k][:].rearrange("p b k -> p (b k)").bitcast(F32), 0, wg)
+                trs += t
+                copies.append(c)
+                quants.append((wg, wc, ws))
+                w_q[k] = (wc, ws)
+            if 0 <= j < NB:
+                tg = work.tile([P, 4 * R], BF16, name="tg", tag="tg", align_bytes=64)
+                tcd = work.tile([P, R], U32, name="tcd", tag="tcd", align_bytes=64)
+                tsc = work.tile([P, R], U8, name="tsc", tag="tsc", align_bytes=64)
+                for h in (0, 1):
+                    t, c = half(t2_sb[j][:].bitcast(F32), h, tg)
+                    trs += t
+                    copies.append(c)
+                quants.append((tg, tcd, tsc))
+                t2_q[j] = (tcd, tsc)
+            if i == 2:
+                t, c = half(c_raw[:].bitcast(F32), 0, c_grouped)
+                trs += t
+                copies.append(c)
+                quants.append((c_grouped, c_codes, c_scales))
+
+            mms = []
+            if 0 <= i < NB:
+                t1 = psum.tile([P, 4, CO], F32, name="t1", tag="t1", bufs=2)
+                t1_ps[i] = t1
+                for t in range(4):
+                    for e in (0, 1):
+                        mms.append(
+                            (t1[:, t, :], a_perm[:, e, t, :], x1_sb[i // 4][:, i % 4, CO * e : CO * (e + 1)], e == 0, e == 1)
+                        )
+            weave(mms, trs)
+
+            t3 = None
+            if 0 <= i < NB:
+                t3 = psum.tile([P, 4, CO], T3_DT, name="t3", tag="t3", bufs=1)
+                tcd, tsc = t2_q[i]
+                wc, ws = w_q[i // 2]
+                cols = slice(CO * (i % 2), CO * (i % 2 + 1))
+                for t in range(4):
+                    rows = slice(P * t, P * (t + 1))
+                    nc.tensor.matmul_mx(
+                        out=t3[:, t, :],
+                        lhsT=tcd[:, rows].bitcast(FP8X4),
+                        lhsT_scale=tsc[:, rows],
+                        rhs=wc[:, cols].bitcast(FP8X4),
+                        rhs_scale=ws[:, cols],
+                        start=True,
+                        stop=True,
+                    )
+            o_ps = None
+            ko = (i - 4) // 2
+            if i % 2 == 0 and 0 <= ko < NB // 2:
+                o_ps = psum.tile([P, 2, 2 * CO], F32, name="o_ps", tag="tp", bufs=5)
+                hc, hs = h_q[ko]
+                for e in (0, 1):
+                    rows = slice(P * e, P * (e + 1))
+                    nc.tensor.matmul_mx(
+                        out=o_ps[:, e, :],
+                        lhsT=c_codes[:, rows].bitcast(FP8X4),
+                        lhsT_scale=c_scales[:, rows],
+                        rhs=hc[:].bitcast(FP8X4),
+                        rhs_scale=hs[:],
+                        start=True,
+                        stop=True,
+                    )
+
+            for dst, src in copies:
+                nc.scalar.copy(out=dst, in_=src)
+            if t3 is not None:
+                t3c = work.tile([P, 4, CO], T3_DT, name="t3c", tag="t3c")
+                t3_sb[i] = t3c
+                if i % 2 == 0:
+                    nc.scalar.copy(out=t3c[:], in_=t3[:])
+            o_sb = None
+            if o_ps is not None:
+                o_sb = work.tile([P, 2, 2, CO], F32, name="o_sb", tag="o_sb")
+                if ko % 2 == 1:
+                    nc.scalar.copy(
+                        out=o_sb[:].rearrange("p b e c -> p e b c"), in_=o_ps[:].rearrange("p e (b c) -> p e b c", b=2)
+                    )
+
+            if i == -1:
+                nc.vector.tensor_copy(out=a_perm[:], in_=a_raw[:].rearrange("p (e m t) -> p e t m", e=2, t=4))
+            if t3 is not None and i % 2 == 1:
+                nc.vector.tensor_copy(out=t3_sb[i][:], in_=t3[:])
+            for grouped, codes, scales in quants:
+                quantize(grouped, codes, scales)
+            kh = (i - 2) // 2
+            if i % 2 == 0 and 0 <= kh < NB // 2:
+                hc = work.tile([P, 2 * CO], U32, name="hc", tag="hc", align_bytes=64)
+                hs = work.tile([P, 2 * CO], U8, name="hs", tag="hs", align_bytes=64)
+                quantize(h_grouped[kh], hc, hs)
+                h_q[kh] = (hc, hs)
+            if t3 is not None:
+                if i % 2 == 0:
+                    hg = work.tile([P, 2 * CO * 4], BF16, name="hg", tag="hg", align_bytes=64)
+                    h_grouped[i // 2] = hg
+                hg = h_grouped[i // 2]
+                lo = 4 * CO * (i % 2)
+                nc.vector.tensor_tensor(
+                    out=hg[:, lo : lo + 4 * CO].rearrange("p (c t) -> p c t", t=4),
+                    in0=t1_ps[i][:].rearrange("p t c -> p c t"),
+                    in1=t3_sb[i][:].rearrange("p t c -> p c t"),
+                    op=mybir.AluOpType.mult,
+                )
+            if o_ps is not None and ko % 2 == 0:
+                nc.vector.tensor_copy(
+                    out=o_sb[:].rearrange("p b e c -> p e b c"), in_=o_ps[:].rearrange("p e (b c) -> p e b c", b=2)
+                )
+
+            if o_ps is not None:
+                nc.sync.dma_start(
+                    out=out[2 * ko : 2 * ko + 2].rearrange("b (p e) c -> p b (e c)", e=2),
+                    in_=o_sb[:].rearrange("p b e c -> p b (e c)"),
+                )

@@ -14,7 +14,9 @@ FP8X4 = mybir.dt.float8_e4m3fn_x4
 T3_DT = F32
 
 P = 128
-LOOKAHEAD = 2
+NPAIR = NB // 2
+C_TICK = 2
+GROUPS = [(b, 2) for b in range(0, NB - 2, 2)] + [(NB - 2, 1), (NB - 1, 1)]
 
 
 def tile_cptensorproduct_pa_kernel(tc, x1, A, t2, w, C, out):
@@ -26,8 +28,9 @@ def tile_cptensorproduct_pa_kernel(tc, x1, A, t2, w, C, out):
         ctx.enter_context(tc.manual_schedule())
 
         t2_sb = [keep.tile([P, 4 * CV], BF16, name="t2_sb%d" % b, tag="t2_sb%d" % b) for b in range(NB)]
-        w_sb = [keep.tile([P, 2, CV], BF16, name="w_sb%d" % k, tag="w_sb%d" % k) for k in range(NB // 2)]
+        w_sb = [keep.tile([P, 2, CV], BF16, name="w_sb%d" % k, tag="w_sb%d" % k) for k in range(NPAIR)]
         x1_sb = [keep.tile([P, 4, 2 * CO], BF16, name="x1_sb%d" % g, tag="x1_sb%d" % g) for g in range(NB // 4)]
+        o_sb = [keep.tile([P, n, 2, CO], F32, name="o_sb%d" % b, tag="o_sb%d" % b) for b, n in GROUPS]
         a_raw = keep.tile([P, 2 * R], BF16, name="a_raw", tag="a_raw")
         c_raw = keep.tile([P, 2 * R], BF16, name="c_raw", tag="c_raw")
 
@@ -37,8 +40,8 @@ def tile_cptensorproduct_pa_kernel(tc, x1, A, t2, w, C, out):
         load_w(0)
         for b in range(NB):
             nc.sync.dma_start(out=t2_sb[b][:], in_=t2[b].rearrange("(m t) k -> m (t k)", t=4))
-            if b % 2 == 0 and b // 2 + 1 < NB // 2:
-                load_w(b // 2 + 1)
+            if b % 2 == 1 and (b + 1) // 2 < NPAIR:
+                load_w((b + 1) // 2)
             if b == 1:
                 nc.sync.dma_start(out=a_raw[:], in_=A.rearrange("(p e) r -> p (e r)", e=2))
             if b % 4 == 1:
@@ -46,7 +49,7 @@ def tile_cptensorproduct_pa_kernel(tc, x1, A, t2, w, C, out):
                 nc.sync.dma_start(
                     out=x1_sb[g][:], in_=x1[4 * g : 4 * g + 4].rearrange("b (p e) c -> p b (e c)", e=2)
                 )
-            if b == 3:
+            if b == C_TICK + 2:
                 nc.sync.dma_start(out=c_raw[:], in_=C.rearrange("(p e) r -> p (e r)", e=2))
 
         ident = keep.tile([P, P], F32, name="ident", tag="ident")
@@ -69,15 +72,16 @@ def tile_cptensorproduct_pa_kernel(tc, x1, A, t2, w, C, out):
         def quantize(grouped, codes, scales):
             nc.vector.quantize_mx(out=codes[:].bitcast(FP8X4), scales=scales[:], in_=grouped[:])
 
-        def weave(mms, trs):
-            for o, i in trs if not mms else []:
-                nc.tensor.transpose(o, i, ident[:])
-            gaps = len(mms) - 1
-            for n, (o, l, r, first, last) in enumerate(mms):
-                nc.tensor.matmul(o, lhsT=l, rhs=r, start=first, stop=last)
-                if n < gaps:
-                    for o2, i2 in trs[len(trs) * n // gaps : len(trs) * (n + 1) // gaps]:
-                        nc.tensor.transpose(o2, i2, ident[:])
+        def t1_matmuls(b, slots):
+            for t in slots:
+                for e in (0, 1):
+                    nc.tensor.matmul(
+                        t1_ps[b][:, t, :],
+                        lhsT=a_perm[:, e, t, :],
+                        rhs=x1_sb[b // 4][:, b % 4, CO * e : CO * (e + 1)],
+                        start=(e == 0),
+                        stop=(e == 1),
+                    )
 
         t2_q = {}
         w_q = {}
@@ -85,51 +89,15 @@ def tile_cptensorproduct_pa_kernel(tc, x1, A, t2, w, C, out):
         h_q = {}
         t1_ps = {}
         t3_sb = {}
+        w_rest = []
+        quants = []
 
         for i in range(-3, NB + 3):
-            j = i + LOOKAHEAD
-            trs = []
-            copies = []
-            quants = []
-            if i % 2 == 1 and (i + 3) // 2 < NB // 2:
-                k = (i + 3) // 2
-                wg = work.tile([P, 4 * 2 * CO], BF16, name="wg", tag="wg", align_bytes=64)
-                wc = work.tile([P, 2 * CO], U32, name="wc", tag="wc", align_bytes=64)
-                ws = work.tile([P, 2 * CO], U8, name="ws", tag="ws", align_bytes=64)
-                t, c = half(w_sb[k][:].rearrange("p b k -> p (b k)").bitcast(F32), 0, wg)
-                trs += t
-                copies.append(c)
-                quants.append((wg, wc, ws))
-                w_q[k] = (wc, ws)
-            if 0 <= j < NB:
-                tg = work.tile([P, 4 * R], BF16, name="tg", tag="tg", align_bytes=64)
-                tcd = work.tile([P, R], U32, name="tcd", tag="tcd", align_bytes=64)
-                tsc = work.tile([P, R], U8, name="tsc", tag="tsc", align_bytes=64)
-                for h in (0, 1):
-                    t, c = half(t2_sb[j][:].bitcast(F32), h, tg)
-                    trs += t
-                    copies.append(c)
-                quants.append((tg, tcd, tsc))
-                t2_q[j] = (tcd, tsc)
-            if i == 2:
-                t, c = half(c_raw[:].bitcast(F32), 0, c_grouped)
-                trs += t
-                copies.append(c)
-                quants.append((c_grouped, c_codes, c_scales))
-
-            mms = []
-            if 0 <= i < NB:
-                t1 = psum.tile([P, 4, CO], F32, name="t1", tag="t1", bufs=2)
-                t1_ps[i] = t1
-                for t in range(4):
-                    for e in (0, 1):
-                        mms.append(
-                            (t1[:, t, :], a_perm[:, e, t, :], x1_sb[i // 4][:, i % 4, CO * e : CO * (e + 1)], e == 0, e == 1)
-                        )
-            weave(mms, trs)
-
+            j = i + 2
             t3 = None
             if 0 <= i < NB:
+                t1_ps[i] = psum.tile([P, 4, CO], F32, name="t1", tag="t1", bufs=2)
+                t1_matmuls(i, (0, 1))
                 t3 = psum.tile([P, 4, CO], T3_DT, name="t3", tag="t3", bufs=1)
                 tcd, tsc = t2_q[i]
                 wc, ws = w_q[i // 2]
@@ -145,69 +113,103 @@ def tile_cptensorproduct_pa_kernel(tc, x1, A, t2, w, C, out):
                         start=True,
                         stop=True,
                     )
-            o_ps = None
-            ko = (i - 4) // 2
-            if i % 2 == 0 and 0 <= ko < NB // 2:
-                o_ps = psum.tile([P, 2, 2 * CO], F32, name="o_ps", tag="tp", bufs=5)
-                hc, hs = h_q[ko]
-                for e in (0, 1):
-                    rows = slice(P * e, P * (e + 1))
-                    nc.tensor.matmul_mx(
-                        out=o_ps[:, e, :],
-                        lhsT=c_codes[:, rows].bitcast(FP8X4),
-                        lhsT_scale=c_scales[:, rows],
-                        rhs=hc[:].bitcast(FP8X4),
-                        rhs_scale=hs[:],
-                        start=True,
-                        stop=True,
-                    )
+            outs = []
+            for k, (b0, n) in enumerate(GROUPS):
+                if b0 + n + 2 == i:
+                    o_ps = psum.tile([P, 2, n * CO], F32, name="o_ps", tag="tp", bufs=5)
+                    hc, hs = h_q[k]
+                    for e in (0, 1):
+                        rows = slice(P * e, P * (e + 1))
+                        nc.tensor.matmul_mx(
+                            out=o_ps[:, e, :],
+                            lhsT=c_codes[:, rows].bitcast(FP8X4),
+                            lhsT_scale=c_scales[:, rows],
+                            rhs=hc[:].bitcast(FP8X4),
+                            rhs_scale=hs[:],
+                            start=True,
+                            stop=True,
+                        )
+                    outs.append((k, b0, n, o_ps))
+            if 0 <= i < NB:
+                t1_matmuls(i, (2, 3))
 
+            trs = []
+            copies = []
+            done = []
+            for t, c, q in w_rest:
+                trs += t
+                copies.append(c)
+                done.append(q)
+            w_rest = []
+            if 0 <= j < NB:
+                tg = work.tile([P, 4 * R], BF16, name="tg", tag="tg", align_bytes=64)
+                tcd = work.tile([P, R], U32, name="tcd", tag="tcd", align_bytes=64)
+                tsc = work.tile([P, R], U8, name="tsc", tag="tsc", align_bytes=64)
+                for h in (0, 1):
+                    t, c = half(t2_sb[j][:].bitcast(F32), h, tg)
+                    trs += t
+                    copies.append(c)
+                done.append((tg, tcd, tsc))
+                t2_q[j] = (tcd, tsc)
+            if i % 2 == 1 and (i + 3) // 2 < NPAIR:
+                k = (i + 3) // 2
+                wg = work.tile([P, 4 * 2 * CO], BF16, name="wg", tag="wg", align_bytes=64)
+                wc = work.tile([P, 2 * CO], U32, name="wc", tag="wc", align_bytes=64)
+                ws = work.tile([P, 2 * CO], U8, name="ws", tag="ws", align_bytes=64)
+                t, c = half(w_sb[k][:].rearrange("p b k -> p (b k)").bitcast(F32), 0, wg)
+                w_q[k] = (wc, ws)
+                if k == 0:
+                    trs += t
+                    copies.append(c)
+                    done.append((wg, wc, ws))
+                else:
+                    trs += t[:2]
+                    w_rest.append((t[2:], c, (wg, wc, ws)))
+            if i == C_TICK:
+                t, c = half(c_raw[:].bitcast(F32), 0, c_grouped)
+                trs += t
+                copies.append(c)
+                done.append((c_grouped, c_codes, c_scales))
+            for o, s in trs:
+                nc.tensor.transpose(o, s, ident[:])
+
+            if t3 is not None:
+                t3_sb[i] = work.tile([P, 4, CO], T3_DT, name="t3c", tag="t3c")
+                nc.scalar.copy(out=t3_sb[i][:], in_=t3[:])
             for dst, src in copies:
                 nc.scalar.copy(out=dst, in_=src)
-            if t3 is not None:
-                t3c = work.tile([P, 4, CO], T3_DT, name="t3c", tag="t3c")
-                t3_sb[i] = t3c
-                if i % 2 == 0:
-                    nc.scalar.copy(out=t3c[:], in_=t3[:])
-            o_sb = None
-            if o_ps is not None:
-                o_sb = work.tile([P, 2, 2, CO], F32, name="o_sb", tag="o_sb")
-                if ko % 2 == 1:
-                    nc.scalar.copy(
-                        out=o_sb[:].rearrange("p b e c -> p e b c"), in_=o_ps[:].rearrange("p e (b c) -> p e b c", b=2)
-                    )
 
-            if i == -1:
-                nc.vector.tensor_copy(out=a_perm[:], in_=a_raw[:].rearrange("p (e m t) -> p e t m", e=2, t=4))
-            if t3 is not None and i % 2 == 1:
-                nc.vector.tensor_copy(out=t3_sb[i][:], in_=t3[:])
+            for k, (b0, n) in enumerate(GROUPS):
+                if b0 == i - 1:
+                    h_grouped[k] = work.tile([P, n * CO * 4], BF16, name="hg", tag="hg", align_bytes=64)
+                if b0 <= i - 1 < b0 + n:
+                    lo = 4 * CO * (i - 1 - b0)
+                    nc.vector.tensor_tensor(
+                        out=h_grouped[k][:, lo : lo + 4 * CO].rearrange("p (c t) -> p c t", t=4),
+                        in0=t1_ps[i - 1][:].rearrange("p t c -> p c t"),
+                        in1=t3_sb[i - 1][:].rearrange("p t c -> p c t"),
+                        op=mybir.AluOpType.mult,
+                    )
             for grouped, codes, scales in quants:
                 quantize(grouped, codes, scales)
-            kh = (i - 2) // 2
-            if i % 2 == 0 and 0 <= kh < NB // 2:
-                hc = work.tile([P, 2 * CO], U32, name="hc", tag="hc", align_bytes=64)
-                hs = work.tile([P, 2 * CO], U8, name="hs", tag="hs", align_bytes=64)
-                quantize(h_grouped[kh], hc, hs)
-                h_q[kh] = (hc, hs)
-            if t3 is not None:
-                if i % 2 == 0:
-                    hg = work.tile([P, 2 * CO * 4], BF16, name="hg", tag="hg", align_bytes=64)
-                    h_grouped[i // 2] = hg
-                hg = h_grouped[i // 2]
-                lo = 4 * CO * (i % 2)
-                nc.vector.tensor_tensor(
-                    out=hg[:, lo : lo + 4 * CO].rearrange("p (c t) -> p c t", t=4),
-                    in0=t1_ps[i][:].rearrange("p t c -> p c t"),
-                    in1=t3_sb[i][:].rearrange("p t c -> p c t"),
-                    op=mybir.AluOpType.mult,
-                )
-            if o_ps is not None and ko % 2 == 0:
-                nc.vector.tensor_copy(
-                    out=o_sb[:].rearrange("p b e c -> p e b c"), in_=o_ps[:].rearrange("p e (b c) -> p e b c", b=2)
-                )
+            quants = done
+            if i == -1:
+                nc.vector.tensor_copy(out=a_perm[:], in_=a_raw[:].rearrange("p (e m t) -> p e t m", e=2, t=4))
+            for k, (b0, n) in enumerate(GROUPS):
+                if b0 + n + 1 == i:
+                    hc = work.tile([P, n * CO], U32, name="hc", tag="hc", align_bytes=64)
+                    hs = work.tile([P, n * CO], U8, name="hs", tag="hs", align_bytes=64)
+                    quantize(h_grouped[k], hc, hs)
+                    h_q[k] = (hc, hs)
 
-            if o_ps is not None:
+            for k, b0, n, o_ps in outs:
+                dst = o_sb[k][:].rearrange("p b e c -> p e b c")
+                src = o_ps[:].rearrange("p e (b c) -> p e b c", b=n)
+                if i < NB:
+                    nc.vector.tensor_copy(out=dst, in_=src)
+                else:
+                    nc.scalar.copy(out=dst, in_=src)
                 nc.sync.dma_start(
-                    out=out[2 * ko : 2 * ko + 2].rearrange("b (p e) c -> p b (e c)", e=2),
-                    in_=o_sb[:].rearrange("p b e c -> p b (e c)"),
+                    out=out[b0 : b0 + n].rearrange("b (p e) c -> p b (e c)", e=2),
+                    in_=o_sb[k][:].rearrange("p b e c -> p b (e c)"),
                 )

@@ -15,7 +15,8 @@ T3_DT = F32
 
 P = 128
 NPAIR = NB // 2
-C_TICK = 2
+C_TICK = 4
+SORT_FROM = 3
 GROUPS = [(b, 2) for b in range(0, NB - 2, 2)] + [(NB - 2, 1), (NB - 1, 1)]
 
 
@@ -59,13 +60,16 @@ def tile_cptensorproduct_pa_kernel(tc, x1, A, t2, w, C, out):
         c_codes = keep.tile([P, D], U32, name="c_codes", tag="c_codes", align_bytes=64)
         c_scales = keep.tile([P, D], U8, name="c_scales", tag="c_scales", align_bytes=64)
 
-        def half(words, h, grouped):
+        def half(words, h, grouped, ordered=None):
             bank = psum.tile([P, 2, 2, P], F32, name="tp", tag="tp", bufs=5)
             trs = []
             for s in (0, 1):
                 for u in (0, 1):
                     lo = 256 * (2 * h + s)
-                    trs.append((bank[:, s, u, :], words[:, lo + u : lo + 256 : 2]))
+                    if ordered is None:
+                        trs.append((bank[:, s, u, :], words[:, lo + u : lo + 256 : 2]))
+                    else:
+                        trs.append((bank[:, s, u, :], ordered[:, s, u, :]))
             dst = grouped[:].bitcast(F32)[:, 512 * h : 512 * (h + 1)].rearrange("p (s m u) -> p s m u", s=2, u=2)
             return trs, (dst, bank[:].rearrange("p s u m -> p s m u"))
 
@@ -91,13 +95,15 @@ def tile_cptensorproduct_pa_kernel(tc, x1, A, t2, w, C, out):
         t3_sb = {}
         w_rest = []
         quants = []
+        sorted_words = {}
 
         for i in range(-3, NB + 3):
             j = i + 2
             t3 = None
             if 0 <= i < NB:
                 t1_ps[i] = psum.tile([P, 4, CO], F32, name="t1", tag="t1", bufs=2)
-                t1_matmuls(i, (0, 1))
+                before = (0, 1) if i < NB - 1 else ()
+                t1_matmuls(i, before)
                 t3 = psum.tile([P, 4, CO], T3_DT, name="t3", tag="t3", bufs=1)
                 tcd, tsc = t2_q[i]
                 wc, ws = w_q[i // 2]
@@ -115,7 +121,7 @@ def tile_cptensorproduct_pa_kernel(tc, x1, A, t2, w, C, out):
                     )
             outs = []
             for k, (b0, n) in enumerate(GROUPS):
-                if b0 + n + 2 == i:
+                if max(b0 + n + 2, C_TICK + 2) == i:
                     o_ps = psum.tile([P, 2, n * CO], F32, name="o_ps", tag="tp", bufs=5)
                     hc, hs = h_q[k]
                     for e in (0, 1):
@@ -131,7 +137,7 @@ def tile_cptensorproduct_pa_kernel(tc, x1, A, t2, w, C, out):
                         )
                     outs.append((k, b0, n, o_ps))
             if 0 <= i < NB:
-                t1_matmuls(i, (2, 3))
+                t1_matmuls(i, (2, 3) if i < NB - 1 else (0, 1, 2, 3))
 
             trs = []
             copies = []
@@ -146,7 +152,7 @@ def tile_cptensorproduct_pa_kernel(tc, x1, A, t2, w, C, out):
                 tcd = work.tile([P, R], U32, name="tcd", tag="tcd", align_bytes=64)
                 tsc = work.tile([P, R], U8, name="tsc", tag="tsc", align_bytes=64)
                 for h in (0, 1):
-                    t, c = half(t2_sb[j][:].bitcast(F32), h, tg)
+                    t, c = half(t2_sb[j][:].bitcast(F32), h, tg, sorted_words.get((j, h)))
                     trs += t
                     copies.append(c)
                 done.append((tg, tcd, tsc))
@@ -201,6 +207,14 @@ def tile_cptensorproduct_pa_kernel(tc, x1, A, t2, w, C, out):
                     hs = work.tile([P, n * CO], U8, name="hs", tag="hs", align_bytes=64)
                     quantize(h_grouped[k], hc, hs)
                     h_q[k] = (hc, hs)
+
+            if SORT_FROM <= j + 1 < NB:
+                sw = work.tile([P, 2, 2, P], F32, name="sw", tag="sw")
+                nc.vector.tensor_copy(
+                    out=sw[:],
+                    in_=t2_sb[j + 1][:].bitcast(F32)[:, 512:1024].rearrange("p (s m u) -> p s u m", s=2, u=2),
+                )
+                sorted_words[(j + 1, 1)] = sw
 
             for k, b0, n, o_ps in outs:
                 dst = o_sb[k][:].rearrange("p b e c -> p e b c")

from contextlib import ExitStack

import concourse.mybir as mybir
from concourse.masks import make_identity

NB, D, CO, CV, R = 16, 256, 128, 512, 512
FLOPS = 2 * NB * CO * (R * D + R * CV + D * R)

F32 = mybir.dt.float32
BF16 = mybir.dt.bfloat16
U32 = mybir.dt.uint32
U8 = mybir.dt.uint8
FP8X4 = mybir.dt.float8_e4m3fn_x4
T3_DT = F32

P = 128
NPAIR = NB // 2
C_TICK = 4
SORT_FROM = 3
GROUPS = [(b, 2) for b in range(0, NB - 2, 2)] + [(NB - 2, 1), (NB - 1, 1)]


def tile_cptensorproduct_pa_kernel(tc, x1, A, t2, w, C, out):
    nc = tc.nc
    with ExitStack() as ctx:
        keep = ctx.enter_context(tc.tile_pool(name="keep", bufs=1))
        work = ctx.enter_context(tc.tile_pool(name="work", bufs=3))
        psum = ctx.enter_context(tc.psum_pool(name="psum", bufs=1))
        ctx.enter_context(tc.manual_schedule())

        t2_sb = [keep.tile([P, 4 * CV], BF16, name="t2_sb%d" % b, tag="t2_sb%d" % b) for b in range(NB)]
        w_sb = [keep.tile([P, 2, CV], BF16, name="w_sb%d" % k, tag="w_sb%d" % k) for k in range(NPAIR)]
        x1_sb = [keep.tile([P, 4, 2 * CO], BF16, name="x1_sb%d" % g, tag="x1_sb%d" % g) for g in range(NB // 4)]
        o_sb = [keep.tile([P, n, 2, CO], F32, name="o_sb%d" % b, tag="o_sb%d" % b) for b, n in GROUPS]
        a_raw = keep.tile([P, 2 * R], BF16, name="a_raw", tag="a_raw")
        c_raw = keep.tile([P, 2 * R], BF16, name="c_raw", tag="c_raw")

        def load_w(k):
            nc.sync.dma_start(out=w_sb[k][:], in_=w[2 * k : 2 * k + 2].rearrange("b c k -> c b k"))

        load_w(0)
        for b in range(NB):
            nc.sync.dma_start(out=t2_sb[b][:], in_=t2[b].rearrange("(m t) k -> m (t k)", t=4))
            if b % 2 == 1 and (b + 1) // 2 < NPAIR:
                load_w((b + 1) // 2)
            if b == 1:
                nc.sync.dma_start(out=a_raw[:], in_=A.rearrange("(p e) r -> p (e r)", e=2))
            if b % 4 == 1:
                g = b // 4
                nc.sync.dma_start(
                    out=x1_sb[g][:], in_=x1[4 * g : 4 * g + 4].rearrange("b (p e) c -> p b (e c)", e=2)
                )
            if b == C_TICK + 2:
                nc.sync.dma_start(out=c_raw[:], in_=C.rearrange("(p e) r -> p (e r)", e=2))

        ident = keep.tile([P, P], F32, name="ident", tag="ident")
        make_identity(nc, ident[:])
        a_perm = keep.tile([P, 2, 4, P], BF16, name="a_perm", tag="a_perm")
        c_grouped = keep.tile([P, 4 * D], BF16, name="c_grouped", tag="c_grouped", align_bytes=64)
        c_codes = keep.tile([P, D], U32, name="c_codes", tag="c_codes", align_bytes=64)
        c_scales = keep.tile([P, D], U8, name="c_scales", tag="c_scales", align_bytes=64)

        def half(words, h, grouped, ordered=None):
            bank = psum.tile([P, 2, 2, P], F32, name="tp", tag="tp", bufs=5)
            trs = []
            for s in (0, 1):
                for u in (0, 1):
                    lo = 256 * (2 * h + s)
                    if ordered is None:
                        trs.append((bank[:, s, u, :], words[:, lo + u : lo + 256 : 2]))
                    else:
                        trs.append((bank[:, s, u, :], ordered[:, s, u, :]))
            dst = grouped[:].bitcast(F32)[:, 512 * h : 512 * (h + 1)].rearrange("p (s m u) -> p s m u", s=2, u=2)
            return trs, (dst, bank[:].rearrange("p s u m -> p s m u"))

        def quantize(grouped, codes, scales):
            nc.vector.quantize_mx(out=codes[:].bitcast(FP8X4), scales=scales[:], in_=grouped[:])

        def t1_matmuls(b, slots):
            for t in slots:
                for e in (0, 1):
                    nc.tensor.matmul(
                        t1_ps[b][:, t, :],
                        lhsT=a_perm[:, e, t, :],
                        rhs=x1_sb[b // 4][:, b % 4, CO * e : CO * (e + 1)],
                        start=(e == 0),
                        stop=(e == 1),
                    )

        t2_q = {}
        w_q = {}
        h_grouped = {}
        h_q = {}
        t1_ps = {}
        t3_sb = {}
        w_rest = []
        quants = []
        sorted_words = {}

        for i in range(-3, NB + 3):
            j = i + 2
            t3 = None
            if 0 <= i < NB:
                t1_ps[i] = psum.tile([P, 4, CO], F32, name="t1", tag="t1", bufs=2)
                before = (0, 1) if i < NB - 1 else ()
                t1_matmuls(i, before)
                t3 = psum.tile([P, 4, CO], T3_DT, name="t3", tag="t3", bufs=1)
                tcd, tsc = t2_q[i]
                wc, ws = w_q[i // 2]
                cols = slice(CO * (i % 2), CO * (i % 2 + 1))
                for t in range(4):
                    rows = slice(P * t, P * (t + 1))
                    nc.tensor.matmul_mx(
                        out=t3[:, t, :],
                        lhsT=tcd[:, rows].bitcast(FP8X4),
                        lhsT_scale=tsc[:, rows],
                        rhs=wc[:, cols].bitcast(FP8X4),
                        rhs_scale=ws[:, cols],
                        start=True,
                        stop=True,
                    )
            outs = []
            for k, (b0, n) in enumerate(GROUPS):
                if max(b0 + n + 2, C_TICK + 2) == i:
                    o_ps = psum.tile([P, 2, n * CO], F32, name="o_ps", tag="tp", bufs=5)
                    hc, hs = h_q[k]
                    for e in (0, 1):
                        rows = slice(P * e, P * (e + 1))
                        nc.tensor.matmul_mx(
                            out=o_ps[:, e, :],
                            lhsT=c_codes[:, rows].bitcast(FP8X4),
                            lhsT_scale=c_scales[:, rows],
                            rhs=hc[:].bitcast(FP8X4),
                            rhs_scale=hs[:],
                            start=True,
                            stop=True,
                        )
                    outs.append((k, b0, n, o_ps))
            if 0 <= i < NB:
                t1_matmuls(i, (2, 3) if i < NB - 1 else (0, 1, 2, 3))

            trs = []
            copies = []
            done = []
            for t, c, q in w_rest:
                trs += t
                copies.append(c)
                done.append(q)
            w_rest = []
            if 0 <= j < NB:
                tg = work.tile([P, 4 * R], BF16, name="tg", tag="tg", align_bytes=64)
                tcd = work.tile([P, R], U32, name="tcd", tag="tcd", align_bytes=64)
                tsc = work.tile([P, R], U8, name="tsc", tag="tsc", align_bytes=64)
                for h in (0, 1):
                    t, c = half(t2_sb[j][:].bitcast(F32), h, tg, sorted_words.get((j, h)))
                    trs += t
                    copies.append(c)
                done.append((tg, tcd, tsc))
                t2_q[j] = (tcd, tsc)
            if i % 2 == 1 and (i + 3) // 2 < NPAIR:
                k = (i + 3) // 2
                wg = work.tile([P, 4 * 2 * CO], BF16, name="wg", tag="wg", align_bytes=64)
                wc = work.tile([P, 2 * CO], U32, name="wc", tag="wc", align_bytes=64)
                ws = work.tile([P, 2 * CO], U8, name="ws", tag="ws", align_bytes=64)
                t, c = half(w_sb[k][:].rearrange("p b k -> p (b k)").bitcast(F32), 0, wg)
                w_q[k] = (wc, ws)
                if k == 0:
                    trs += t
                    copies.append(c)
                    done.append((wg, wc, ws))
                else:
                    trs += t[:2]
                    w_rest.append((t[2:], c, (wg, wc, ws)))
            if i == C_TICK:
                t, c = half(c_raw[:].bitcast(F32), 0, c_grouped)
                trs += t
                copies.append(c)
                done.append((c_grouped, c_codes, c_scales))
            for o, s in trs:
                nc.tensor.transpose(o, s, ident[:])

            if t3 is not None:
                t3_sb[i] = work.tile([P, 4, CO], T3_DT, name="t3c", tag="t3c")
                nc.scalar.copy(out=t3_sb[i][:], in_=t3[:])
            for dst, src in copies:
                nc.scalar.copy(out=dst, in_=src)

            for k, (b0, n) in enumerate(GROUPS):
                if b0 == i - 1:
                    h_grouped[k] = work.tile([P, n * CO * 4], BF16, name="hg", tag="hg", align_bytes=64)
                if b0 <= i - 1 < b0 + n:
                    lo = 4 * CO * (i - 1 - b0)
                    nc.vector.tensor_tensor(
                        out=h_grouped[k][:, lo : lo + 4 * CO].rearrange("p (c t) -> p c t", t=4),
                        in0=t1_ps[i - 1][:].rearrange("p t c -> p c t"),
                        in1=t3_sb[i - 1][:].rearrange("p t c -> p c t"),
                        op=mybir.AluOpType.mult,
                    )
            for grouped, codes, scales in quants:
                quantize(grouped, codes, scales)
            quants = done
            if i == -1:
                nc.vector.tensor_copy(out=a_perm[:], in_=a_raw[:].rearrange("p (e m t) -> p e t m", e=2, t=4))
            for k, (b0, n) in enumerate(GROUPS):
                if b0 + n + 1 == i:
                    hc = work.tile([P, n * CO], U32, name="hc", tag="hc", align_bytes=64)
                    hs = work.tile([P, n * CO], U8, name="hs", tag="hs", align_bytes=64)
                    quantize(h_grouped[k], hc, hs)
                    h_q[k] = (hc, hs)

            if SORT_FROM <= j + 1 < NB:
                sw = work.tile([P, 2, 2, P], F32, name="sw", tag="sw")
                nc.vector.tensor_copy(
                    out=sw[:],
                    in_=t2_sb[j + 1][:].bitcast(F32)[:, 512:1024].rearrange("p (s m u) -> p s u m", s=2, u=2),
                )
                sorted_words[(j + 1, 1)] = sw

            for k, b0, n, o_ps in outs:
                dst = o_sb[k][:].rearrange("p b e c -> p e b c")
                src = o_ps[:].rearrange("p e (b c) -> p e b c", b=n)
                if i < NB:
                    nc.vector.tensor_copy(out=dst, in_=src)
                else:
                    nc.scalar.copy(out=dst, in_=src)
                nc.sync.dma_start(
                    out=out[b0 : b0 + n].rearrange("b (p e) c -> p b (e c)", e=2),
                    in_=o_sb[k][:].rearrange("p b e c -> p b (e c)"),
                )
